import numpy as np
import ml_dtypes

BF16 = ml_dtypes.bfloat16


def bf(x):
    return np.asarray(x, np.float32).astype(BF16)


def f32(x):
    return np.asarray(x, np.float32)


def f64(x):
    return np.asarray(x).astype(np.float64)


def striped(idx):
    return np.tile(idx.reshape(-1, 16).T, (8, 1))


C, S, N = 512, 1024, 512
RES = 0.5


def sigmoid(v):
    return 1.0 / (1.0 + np.exp(-v))


def setup_inputs():
    return {"base": f32(np.random.standard_normal((C, S))), "h": bf(np.random.standard_normal((C, N))), "w_gate": bf(np.random.standard_normal((C, C)) / np.sqrt(C)), "b_gate": f32(0.5 * np.random.standard_normal((C, 1))), "w_fuse": bf(np.random.standard_normal((C, C)) / np.sqrt(C)), "b_fuse": f32(0.5 * np.random.standard_normal((C, 1))), "offs": striped(np.random.permutation(S)[:N])}


def reference(base, h, w_gate, b_gate, w_fuse, b_fuse, offs):
    idx = offs[:16].T.reshape(-1)
    x = f64(h)
    gate = sigmoid(f64(w_gate).T @ x + f64(b_gate))
    v = f64(w_fuse).T @ x + f64(b_fuse)
    fused = v * sigmoid(v)
    out = f64(base).copy()
    out[:, idx] = x + RES * gate * fused
    return out

@@ -1,0 +1,70 @@
+import concourse.mybir as mybir
+
+P = 128
+C = 512
+S = 1024
+N = 512
+CB = C // P
+
+FLOPS = 2 * 2 * C * C * N
+
+BF16, F32, U16 = mybir.dt.bfloat16, mybir.dt.float32, mybir.dt.uint16
+MULT, ADD = mybir.AluOpType.mult, mybir.AluOpType.add
+SIGMOID = mybir.ActivationFunctionType.Sigmoid
+SILU = mybir.ActivationFunctionType.Silu
+
+
+def tile_centergeoattention_kernel(tc, base, h, w_gate, b_gate, w_fuse, b_fuse, offs, out):
+    nc = tc.nc
+    with (
+        tc.tile_pool(name="held", bufs=1) as held,
+        tc.tile_pool(name="work", bufs=2) as work,
+        tc.psum_pool(name="psum", bufs=CB) as psum,
+    ):
+        offsets = held.tile([P, N // 16], U16, name="offsets")
+        nc.sync.dma_start(offsets[:], offs)
+
+        gate_bias = held.tile([P, CB], F32, name="gate_bias")
+        fuse_bias = held.tile([P, CB], F32, name="fuse_bias")
+        with nc.allow_non_contiguous_dma(reason="two bias columns, one element to a partition"):
+            nc.gpsimd.dma_start(gate_bias[:], b_gate.rearrange("(cb p) o -> p (cb o)", p=P))
+            nc.gpsimd.dma_start(fuse_bias[:], b_fuse.rearrange("(cb p) o -> p (cb o)", p=P))
+
+        queues = [nc.sync, nc.scalar]
+        loads = []
+        h_bf, gate_w, fuse_w, window = [], [], [], []
+        for kb in range(CB):
+            rows = slice(kb * P, (kb + 1) * P)
+            h_bf.append(held.tile([P, N], BF16, name=f"h_bf{kb}"))
+            gate_w.append(held.tile([P, C], BF16, name=f"gate_w{kb}"))
+            fuse_w.append(held.tile([P, C], BF16, name=f"fuse_w{kb}"))
+            loads += [(h_bf[kb], h[rows, :]), (gate_w[kb], w_gate[rows, :]), (fuse_w[kb], w_fuse[rows, :])]
+        for cb in range(CB):
+            window.append(held.tile([P, S], F32, name=f"window{cb}"))
+            loads.append((window[cb], base[cb * P : (cb + 1) * P, :]))
+        for i, (dst, src) in enumerate(loads):
+            queues[i % 2].dma_start(dst[:], src)
+
+        h_f32 = []
+        for cb in range(CB):
+            h_f32.append(held.tile([P, N], F32, name=f"h_f32_{cb}"))
+            nc.vector.tensor_copy(h_f32[cb][:], h_bf[cb][:])
+
+        for cb in range(CB):
+            cols = slice(cb * P, (cb + 1) * P)
+            gate_ps = psum.tile([P, N], F32, name="gate_ps")
+            fuse_ps = psum.tile([P, N], F32, name="fuse_ps")
+            for kb in range(CB):
+                nc.tensor.matmul(gate_ps[:], gate_w[kb][:, cols], h_bf[kb][:], start=kb == 0, stop=kb == CB - 1)
+                nc.tensor.matmul(fuse_ps[:], fuse_w[kb][:, cols], h_bf[kb][:], start=kb == 0, stop=kb == CB - 1)
+
+            gate = work.tile([P, N], F32, name="gate")
+            fused = work.tile([P, N], F32, name="fused")
+            nc.scalar.activation(gate[:], gate_ps[:], SIGMOID, bias=gate_bias[:, cb : cb + 1])
+            nc.scalar.activation(fused[:], fuse_ps[:], SILU, bias=fuse_bias[:, cb : cb + 1])
+
+            update = work.tile([P, N], F32, name="update")
+            nc.vector.scalar_tensor_tensor(update[:], gate[:], 0.5, fused[:], MULT, MULT)
+
+            nc.vector.tensor_tensor(window[cb][:].indirect(offsets[:]), h_f32[cb][:], update[:], ADD)
+            nc.sync.dma_start(out[cb * P : (cb + 1) * P, :], window[cb][:])

@@ -10,8 +10,9 @@ FLOPS = 2 * 2 * C * C * N
 
 BF16, F32, U16 = mybir.dt.bfloat16, mybir.dt.float32, mybir.dt.uint16
 MULT, ADD = mybir.AluOpType.mult, mybir.AluOpType.add
-SIGMOID = mybir.ActivationFunctionType.Sigmoid
+TANH = mybir.ActivationFunctionType.Tanh
 SILU = mybir.ActivationFunctionType.Silu
+COPY = mybir.ActivationFunctionType.Copy
 
 
 def tile_centergeoattention_kernel(tc, base, h, w_gate, b_gate, w_fuse, b_fuse, offs, out):
@@ -27,23 +28,25 @@ def tile_centergeoattention_kernel(tc, base, h, w_gate, b_gate, w_fuse, b_fuse, 
         gate_bias = held.tile([P, CB], F32, name="gate_bias")
         fuse_bias = held.tile([P, CB], F32, name="fuse_bias")
         with nc.allow_non_contiguous_dma(reason="two bias columns, one element to a partition"):
-            nc.gpsimd.dma_start(gate_bias[:], b_gate.rearrange("(cb p) o -> p (cb o)", p=P))
-            nc.gpsimd.dma_start(fuse_bias[:], b_fuse.rearrange("(cb p) o -> p (cb o)", p=P))
+            nc.scalar.dma_start(gate_bias[:], b_gate.rearrange("(cb p) o -> p (cb o)", p=P))
+            nc.scalar.dma_start(fuse_bias[:], b_fuse.rearrange("(cb p) o -> p (cb o)", p=P))
 
-        queues = [nc.sync, nc.scalar]
-        loads = []
         h_bf, gate_w, fuse_w, window = [], [], [], []
         for kb in range(CB):
             rows = slice(kb * P, (kb + 1) * P)
             h_bf.append(held.tile([P, N], BF16, name=f"h_bf{kb}"))
             gate_w.append(held.tile([P, C], BF16, name=f"gate_w{kb}"))
+            nc.sync.dma_start(h_bf[kb][:], h[rows, :])
+            nc.sync.dma_start(gate_w[kb][:], w_gate[rows, :])
+        for kb in range(CB):
             fuse_w.append(held.tile([P, C], BF16, name=f"fuse_w{kb}"))
-            loads += [(h_bf[kb], h[rows, :]), (gate_w[kb], w_gate[rows, :]), (fuse_w[kb], w_fuse[rows, :])]
+            nc.sync.dma_start(fuse_w[kb][:], w_fuse[kb * P : (kb + 1) * P, :])
         for cb in range(CB):
             window.append(held.tile([P, S], F32, name=f"window{cb}"))
-            loads.append((window[cb], base[cb * P : (cb + 1) * P, :]))
-        for i, (dst, src) in enumerate(loads):
-            queues[i % 2].dma_start(dst[:], src)
+            nc.sync.dma_start(window[cb][:], base[cb * P : (cb + 1) * P, :])
+
+        half_gate_bias = held.tile([P, CB], F32, name="half_gate_bias")
+        nc.vector.tensor_scalar_mul(half_gate_bias[:], gate_bias[:], 0.5)
 
         h_f32 = []
         for cb in range(CB):
@@ -53,18 +56,21 @@ def tile_centergeoattention_kernel(tc, base, h, w_gate, b_gate, w_fuse, b_fuse, 
         for cb in range(CB):
             cols = slice(cb * P, (cb + 1) * P)
             gate_ps = psum.tile([P, N], F32, name="gate_ps")
-            fuse_ps = psum.tile([P, N], F32, name="fuse_ps")
             for kb in range(CB):
                 nc.tensor.matmul(gate_ps[:], gate_w[kb][:, cols], h_bf[kb][:], start=kb == 0, stop=kb == CB - 1)
+            fuse_ps = psum.tile([P, N], F32, name="fuse_ps")
+            for kb in range(CB):
                 nc.tensor.matmul(fuse_ps[:], fuse_w[kb][:, cols], h_bf[kb][:], start=kb == 0, stop=kb == CB - 1)
 
-            gate = work.tile([P, N], F32, name="gate")
+            gate_tanh = work.tile([P, N], F32, name="gate_tanh")
+            half_gate = work.tile([P, N], F32, name="half_gate")
             fused = work.tile([P, N], F32, name="fused")
-            nc.scalar.activation(gate[:], gate_ps[:], SIGMOID, bias=gate_bias[:, cb : cb + 1])
+            nc.scalar.activation(gate_tanh[:], gate_ps[:], TANH, bias=half_gate_bias[:, cb : cb + 1], scale=0.5)
+            nc.scalar.activation(half_gate[:], gate_tanh[:], COPY, bias=0.25, scale=0.25)
             nc.scalar.activation(fused[:], fuse_ps[:], SILU, bias=fuse_bias[:, cb : cb + 1])
 
             update = work.tile([P, N], F32, name="update")
-            nc.vector.scalar_tensor_tensor(update[:], gate[:], 0.5, fused[:], MULT, MULT)
+            nc.vector.tensor_tensor(update[:], half_gate[:], fused[:], MULT)
 
             nc.vector.tensor_tensor(window[cb][:].indirect(offsets[:]), h_f32[cb][:], update[:], ADD)
             nc.sync.dma_start(out[cb * P : (cb + 1) * P, :], window[cb][:])

@@ -27,23 +27,34 @@ def tile_centergeoattention_kernel(tc, base, h, w_gate, b_gate, w_fuse, b_fuse, 
 
         gate_bias = held.tile([P, CB], F32, name="gate_bias")
         fuse_bias = held.tile([P, CB], F32, name="fuse_bias")
-        with nc.allow_non_contiguous_dma(reason="two bias columns, one element to a partition"):
-            nc.scalar.dma_start(gate_bias[:], b_gate.rearrange("(cb p) o -> p (cb o)", p=P))
-            nc.scalar.dma_start(fuse_bias[:], b_fuse.rearrange("(cb p) o -> p (cb o)", p=P))
+        h_bf = [held.tile([P, N], BF16, name=f"h_bf{kb}") for kb in range(CB)]
+        gate_w = [held.tile([P, CB, P], BF16, name=f"gate_w{cb}") for cb in range(CB)]
+        fuse_w = [held.tile([P, CB, P], BF16, name=f"fuse_w{cb}") for cb in range(CB)]
+        window = [held.tile([P, S], F32, name=f"window{cb}") for cb in range(CB)]
 
-        h_bf, gate_w, fuse_w, window = [], [], [], []
+        def load_bias(queue, tile, bias):
+            with nc.allow_non_contiguous_dma(reason="a bias column, one element to a partition"):
+                queue.dma_start(tile[:], bias.rearrange("(cb p) o -> p (cb o)", p=P))
+
+        def load_weight(queue, tile, weight, cb):
+            queue.dma_start(tile[:], weight[:, cb * P : (cb + 1) * P].rearrange("(kb p) m -> p kb m", p=P))
+
+        load_bias(nc.sync, gate_bias, b_gate)
+        load_weight(nc.scalar, gate_w[0], w_gate, 0)
         for kb in range(CB):
-            rows = slice(kb * P, (kb + 1) * P)
-            h_bf.append(held.tile([P, N], BF16, name=f"h_bf{kb}"))
-            gate_w.append(held.tile([P, C], BF16, name=f"gate_w{kb}"))
-            nc.sync.dma_start(h_bf[kb][:], h[rows, :])
-            nc.sync.dma_start(gate_w[kb][:], w_gate[rows, :])
-        for kb in range(CB):
-            fuse_w.append(held.tile([P, C], BF16, name=f"fuse_w{kb}"))
-            nc.sync.dma_start(fuse_w[kb][:], w_fuse[kb * P : (kb + 1) * P, :])
-        for cb in range(CB):
-            window.append(held.tile([P, S], F32, name=f"window{cb}"))
+            queue = nc.sync if kb % 2 == 0 else nc.scalar
+            queue.dma_start(h_bf[kb][:], h[kb * P : (kb + 1) * P, :])
+        load_weight(nc.sync, fuse_w[0], w_fuse, 0)
+        load_bias(nc.scalar, fuse_bias, b_fuse)
+        nc.sync.dma_start(window[0][:], base[0:P, :])
+        for cb in range(1, CB):
+            load_weight(nc.sync, gate_w[cb], w_gate, cb)
+            load_weight(nc.sync, fuse_w[cb], w_fuse, cb)
             nc.sync.dma_start(window[cb][:], base[cb * P : (cb + 1) * P, :])
+
+        scratch = held.tile([P, 1], F32, name="scratch")
+        nc.vector.memset(scratch[:], 0.0)
+        nc.scalar.activation(scratch[:], scratch[:], TANH)
 
         half_gate_bias = held.tile([P, CB], F32, name="half_gate_bias")
         nc.vector.tensor_scalar_mul(half_gate_bias[:], gate_bias[:], 0.5)
@@ -54,13 +65,12 @@ def tile_centergeoattention_kernel(tc, base, h, w_gate, b_gate, w_fuse, b_fuse, 
             nc.vector.tensor_copy(h_f32[cb][:], h_bf[cb][:])
 
         for cb in range(CB):
-            cols = slice(cb * P, (cb + 1) * P)
             gate_ps = psum.tile([P, N], F32, name="gate_ps")
             for kb in range(CB):
-                nc.tensor.matmul(gate_ps[:], gate_w[kb][:, cols], h_bf[kb][:], start=kb == 0, stop=kb == CB - 1)
+                nc.tensor.matmul(gate_ps[:], gate_w[cb][:, kb, :], h_bf[kb][:], start=kb == 0, stop=kb == CB - 1)
             fuse_ps = psum.tile([P, N], F32, name="fuse_ps")
             for kb in range(CB):
-                nc.tensor.matmul(fuse_ps[:], fuse_w[kb][:, cols], h_bf[kb][:], start=kb == 0, stop=kb == CB - 1)
+                nc.tensor.matmul(fuse_ps[:], fuse_w[cb][:, kb, :], h_bf[kb][:], start=kb == 0, stop=kb == CB - 1)
 
             gate_tanh = work.tile([P, N], F32, name="gate_tanh")
             half_gate = work.tile([P, N], F32, name="half_gate")

@@ -5,6 +5,7 @@ C = 512
 S = 1024
 N = 512
 CB = C // P
+WARM_MATMULS = 5
 
 FLOPS = 2 * 2 * C * C * N
 
@@ -20,41 +21,43 @@ def tile_centergeoattention_kernel(tc, base, h, w_gate, b_gate, w_fuse, b_fuse, 
     with (
         tc.tile_pool(name="held", bufs=1) as held,
         tc.tile_pool(name="work", bufs=2) as work,
-        tc.psum_pool(name="psum", bufs=CB) as psum,
+        tc.psum_pool(name="psum", bufs=1) as psum,
     ):
         offsets = held.tile([P, N // 16], U16, name="offsets")
-        nc.sync.dma_start(offsets[:], offs)
-
         gate_bias = held.tile([P, CB], F32, name="gate_bias")
         fuse_bias = held.tile([P, CB], F32, name="fuse_bias")
-        h_bf = [held.tile([P, N], BF16, name=f"h_bf{kb}") for kb in range(CB)]
-        gate_w = [held.tile([P, CB, P], BF16, name=f"gate_w{cb}") for cb in range(CB)]
-        fuse_w = [held.tile([P, CB, P], BF16, name=f"fuse_w{cb}") for cb in range(CB)]
+        h_half = [held.tile([P, 2, N], BF16, name=f"h_half{i}") for i in range(2)]
+        gate_w_half = [held.tile([P, 2, C], BF16, name=f"gate_w_half{i}") for i in range(2)]
+        fuse_w_half = [held.tile([P, 2, C], BF16, name=f"fuse_w_half{i}") for i in range(2)]
         window = [held.tile([P, S], F32, name=f"window{cb}") for cb in range(CB)]
 
         def load_bias(queue, tile, bias):
             with nc.allow_non_contiguous_dma(reason="a bias column, one element to a partition"):
                 queue.dma_start(tile[:], bias.rearrange("(cb p) o -> p (cb o)", p=P))
 
-        def load_weight(queue, tile, weight, cb):
-            queue.dma_start(tile[:], weight[:, cb * P : (cb + 1) * P].rearrange("(kb p) m -> p kb m", p=P))
+        def load_half(queue, halves, rows, i):
+            queue.dma_start(halves[i][:], rows[2 * i * P : 2 * (i + 1) * P, :].rearrange("(j p) n -> p j n", p=P))
 
         load_bias(nc.sync, gate_bias, b_gate)
-        load_weight(nc.scalar, gate_w[0], w_gate, 0)
-        for kb in range(CB):
-            queue = nc.sync if kb % 2 == 0 else nc.scalar
-            queue.dma_start(h_bf[kb][:], h[kb * P : (kb + 1) * P, :])
-        load_weight(nc.sync, fuse_w[0], w_fuse, 0)
         load_bias(nc.scalar, fuse_bias, b_fuse)
-        nc.sync.dma_start(window[0][:], base[0:P, :])
-        for cb in range(1, CB):
-            load_weight(nc.sync, gate_w[cb], w_gate, cb)
-            load_weight(nc.sync, fuse_w[cb], w_fuse, cb)
+        for i in range(2):
+            load_half(nc.sync, h_half, h, i)
+            load_half(nc.scalar, gate_w_half, w_gate, i)
+        load_half(nc.sync, fuse_w_half, w_fuse, 0)
+        load_half(nc.scalar, fuse_w_half, w_fuse, 1)
+        nc.sync.dma_start(offsets[:], offs)
+        for cb in range(CB):
             nc.sync.dma_start(window[cb][:], base[cb * P : (cb + 1) * P, :])
 
+        zeros = held.tile([P, N], BF16, name="zeros")
+        nc.gpsimd.memset(zeros[:], 0.0)
+        warm_ps = psum.tile([P, N], F32, name="warm_ps")
+        for i in range(WARM_MATMULS):
+            nc.tensor.matmul(warm_ps[:], zeros[:, 0:P], zeros[:], start=True, stop=True)
+
         scratch = held.tile([P, 1], F32, name="scratch")
-        nc.vector.memset(scratch[:], 0.0)
-        nc.scalar.activation(scratch[:], scratch[:], TANH)
+        nc.gpsimd.memset(scratch[:], 0.0)
+        nc.scalar.activation(scratch[:], scratch[:], SILU)
 
         half_gate_bias = held.tile([P, CB], F32, name="half_gate_bias")
         nc.vector.tensor_scalar_mul(half_gate_bias[:], gate_bias[:], 0.5)
@@ -62,15 +65,23 @@ def tile_centergeoattention_kernel(tc, base, h, w_gate, b_gate, w_fuse, b_fuse, 
         h_f32 = []
         for cb in range(CB):
             h_f32.append(held.tile([P, N], F32, name=f"h_f32_{cb}"))
-            nc.vector.tensor_copy(h_f32[cb][:], h_bf[cb][:])
+            nc.vector.tensor_copy(h_f32[cb][:], h_half[cb // 2][:, cb % 2, :])
+
+        def product(acc, w_half, cb):
+            for kb in range(CB):
+                nc.tensor.matmul(
+                    acc[:],
+                    w_half[kb // 2][:, kb % 2, cb * P : (cb + 1) * P],
+                    h_half[kb // 2][:, kb % 2, :],
+                    start=kb == 0,
+                    stop=kb == CB - 1,
+                )
 
         for cb in range(CB):
             gate_ps = psum.tile([P, N], F32, name="gate_ps")
-            for kb in range(CB):
-                nc.tensor.matmul(gate_ps[:], gate_w[cb][:, kb, :], h_bf[kb][:], start=kb == 0, stop=kb == CB - 1)
+            product(gate_ps, gate_w_half, cb)
             fuse_ps = psum.tile([P, N], F32, name="fuse_ps")
-            for kb in range(CB):
-                nc.tensor.matmul(fuse_ps[:], fuse_w[cb][:, kb, :], h_bf[kb][:], start=kb == 0, stop=kb == CB - 1)
+            product(fuse_ps, fuse_w_half, cb)
 
             gate_tanh = work.tile([P, N], F32, name="gate_tanh")
             half_gate = work.tile([P, N], F32, name="half_gate")

@@ -26,27 +26,30 @@ def tile_centergeoattention_kernel(tc, base, h, w_gate, b_gate, w_fuse, b_fuse, 
         offsets = held.tile([P, N // 16], U16, name="offsets")
         gate_bias = held.tile([P, CB], F32, name="gate_bias")
         fuse_bias = held.tile([P, CB], F32, name="fuse_bias")
-        h_half = [held.tile([P, 2, N], BF16, name=f"h_half{i}") for i in range(2)]
-        gate_w_half = [held.tile([P, 2, C], BF16, name=f"gate_w_half{i}") for i in range(2)]
-        fuse_w_half = [held.tile([P, 2, C], BF16, name=f"fuse_w_half{i}") for i in range(2)]
+        h_bf = [held.tile([P, N], BF16, name=f"h_bf{kb}") for kb in range(CB)]
+        gate_w = [held.tile([P, CB, P], BF16, name=f"gate_w{cb}") for cb in range(CB)]
+        fuse_w = [held.tile([P, CB, P], BF16, name=f"fuse_w{cb}") for cb in range(CB)]
         window = [held.tile([P, S], F32, name=f"window{cb}") for cb in range(CB)]
 
         def load_bias(queue, tile, bias):
             with nc.allow_non_contiguous_dma(reason="a bias column, one element to a partition"):
                 queue.dma_start(tile[:], bias.rearrange("(cb p) o -> p (cb o)", p=P))
 
-        def load_half(queue, halves, rows, i):
-            queue.dma_start(halves[i][:], rows[2 * i * P : 2 * (i + 1) * P, :].rearrange("(j p) n -> p j n", p=P))
+        def load_weight(queue, tile, weight, cb):
+            queue.dma_start(tile[:], weight[:, cb * P : (cb + 1) * P].rearrange("(kb p) m -> p kb m", p=P))
 
+        load_weight(nc.scalar, gate_w[0], w_gate, 0)
+        for kb in range(CB):
+            queue = nc.sync if kb % 2 == 0 else nc.scalar
+            queue.dma_start(h_bf[kb][:], h[kb * P : (kb + 1) * P, :])
         load_bias(nc.sync, gate_bias, b_gate)
+        load_weight(nc.sync, fuse_w[0], w_fuse, 0)
         load_bias(nc.scalar, fuse_bias, b_fuse)
-        for i in range(2):
-            load_half(nc.sync, h_half, h, i)
-            load_half(nc.scalar, gate_w_half, w_gate, i)
-        load_half(nc.sync, fuse_w_half, w_fuse, 0)
-        load_half(nc.scalar, fuse_w_half, w_fuse, 1)
         nc.sync.dma_start(offsets[:], offs)
-        for cb in range(CB):
+        nc.sync.dma_start(window[0][:], base[0:P, :])
+        for cb in range(1, CB):
+            load_weight(nc.sync, gate_w[cb], w_gate, cb)
+            load_weight(nc.sync, fuse_w[cb], w_fuse, cb)
             nc.sync.dma_start(window[cb][:], base[cb * P : (cb + 1) * P, :])
 
         zeros = held.tile([P, N], BF16, name="zeros")
@@ -65,23 +68,17 @@ def tile_centergeoattention_kernel(tc, base, h, w_gate, b_gate, w_fuse, b_fuse, 
         h_f32 = []
         for cb in range(CB):
             h_f32.append(held.tile([P, N], F32, name=f"h_f32_{cb}"))
-            nc.vector.tensor_copy(h_f32[cb][:], h_half[cb // 2][:, cb % 2, :])
+            nc.vector.tensor_copy(h_f32[cb][:], h_bf[cb][:])
 
-        def product(acc, w_half, cb):
+        def product(acc, weight_block):
             for kb in range(CB):
-                nc.tensor.matmul(
-                    acc[:],
-                    w_half[kb // 2][:, kb % 2, cb * P : (cb + 1) * P],
-                    h_half[kb // 2][:, kb % 2, :],
-                    start=kb == 0,
-                    stop=kb == CB - 1,
-                )
+                nc.tensor.matmul(acc[:], weight_block[:, kb, :], h_bf[kb][:], start=kb == 0, stop=kb == CB - 1)
 
         for cb in range(CB):
             gate_ps = psum.tile([P, N], F32, name="gate_ps")
-            product(gate_ps, gate_w_half, cb)
+            product(gate_ps, gate_w[cb])
             fuse_ps = psum.tile([P, N], F32, name="fuse_ps")
-            product(fuse_ps, fuse_w_half, cb)
+            product(fuse_ps, fuse_w[cb])
 
             gate_tanh = work.tile([P, N], F32, name="gate_tanh")
             half_gate = work.tile([P, N], F32, name="half_gate")

@@ -24,16 +24,15 @@ def tile_centergeoattention_kernel(tc, base, h, w_gate, b_gate, w_fuse, b_fuse, 
         tc.psum_pool(name="psum", bufs=1) as psum,
     ):
         offsets = held.tile([P, N // 16], U16, name="offsets")
-        gate_bias = held.tile([P, CB], F32, name="gate_bias")
-        fuse_bias = held.tile([P, CB], F32, name="fuse_bias")
+        gate_bias = [held.tile([P, 1], F32, name=f"gate_bias{cb}") for cb in range(CB)]
+        fuse_bias = [held.tile([P, 1], F32, name=f"fuse_bias{cb}") for cb in range(CB)]
         h_bf = [held.tile([P, N], BF16, name=f"h_bf{kb}") for kb in range(CB)]
         gate_w = [held.tile([P, CB, P], BF16, name=f"gate_w{cb}") for cb in range(CB)]
         fuse_w = [held.tile([P, CB, P], BF16, name=f"fuse_w{cb}") for cb in range(CB)]
         window = [held.tile([P, S], F32, name=f"window{cb}") for cb in range(CB)]
 
-        def load_bias(queue, tile, bias):
-            with nc.allow_non_contiguous_dma(reason="a bias column, one element to a partition"):
-                queue.dma_start(tile[:], bias.rearrange("(cb p) o -> p (cb o)", p=P))
+        def load_bias(queue, tile, bias, cb):
+            queue.dma_start(tile[:], bias[cb * P : (cb + 1) * P, :])
 
         def load_weight(queue, tile, weight, cb):
             queue.dma_start(tile[:], weight[:, cb * P : (cb + 1) * P].rearrange("(kb p) m -> p kb m", p=P))
@@ -42,12 +41,14 @@ def tile_centergeoattention_kernel(tc, base, h, w_gate, b_gate, w_fuse, b_fuse, 
         for kb in range(CB):
             queue = nc.sync if kb % 2 == 0 else nc.scalar
             queue.dma_start(h_bf[kb][:], h[kb * P : (kb + 1) * P, :])
-        load_bias(nc.sync, gate_bias, b_gate)
+        load_bias(nc.sync, gate_bias[0], b_gate, 0)
         load_weight(nc.sync, fuse_w[0], w_fuse, 0)
-        load_bias(nc.scalar, fuse_bias, b_fuse)
+        load_bias(nc.scalar, fuse_bias[0], b_fuse, 0)
         nc.sync.dma_start(offsets[:], offs)
         nc.sync.dma_start(window[0][:], base[0:P, :])
         for cb in range(1, CB):
+            load_bias(nc.sync, gate_bias[cb], b_gate, cb)
+            load_bias(nc.sync, fuse_bias[cb], b_fuse, cb)
             load_weight(nc.sync, gate_w[cb], w_gate, cb)
             load_weight(nc.sync, fuse_w[cb], w_fuse, cb)
             nc.sync.dma_start(window[cb][:], base[cb * P : (cb + 1) * P, :])
@@ -61,9 +62,6 @@ def tile_centergeoattention_kernel(tc, base, h, w_gate, b_gate, w_fuse, b_fuse, 
         scratch = held.tile([P, 1], F32, name="scratch")
         nc.gpsimd.memset(scratch[:], 0.0)
         nc.scalar.activation(scratch[:], scratch[:], SILU)
-
-        half_gate_bias = held.tile([P, CB], F32, name="half_gate_bias")
-        nc.vector.tensor_scalar_mul(half_gate_bias[:], gate_bias[:], 0.5)
 
         h_f32 = []
         for cb in range(CB):
@@ -80,12 +78,14 @@ def tile_centergeoattention_kernel(tc, base, h, w_gate, b_gate, w_fuse, b_fuse, 
             fuse_ps = psum.tile([P, N], F32, name="fuse_ps")
             product(fuse_ps, fuse_w[cb])
 
+            half_gate_bias = work.tile([P, 1], F32, name="half_gate_bias")
+            nc.scalar.mul(half_gate_bias[:], gate_bias[cb][:], 0.5)
             gate_tanh = work.tile([P, N], F32, name="gate_tanh")
             half_gate = work.tile([P, N], F32, name="half_gate")
             fused = work.tile([P, N], F32, name="fused")
-            nc.scalar.activation(gate_tanh[:], gate_ps[:], TANH, bias=half_gate_bias[:, cb : cb + 1], scale=0.5)
+            nc.scalar.activation(gate_tanh[:], gate_ps[:], TANH, bias=half_gate_bias[:], scale=0.5)
             nc.scalar.activation(half_gate[:], gate_tanh[:], COPY, bias=0.25, scale=0.25)
-            nc.scalar.activation(fused[:], fuse_ps[:], SILU, bias=fuse_bias[:, cb : cb + 1])
+            nc.scalar.activation(fused[:], fuse_ps[:], SILU, bias=fuse_bias[cb][:])
 
             update = work.tile([P, N], F32, name="update")
             nc.vector.tensor_tensor(update[:], half_gate[:], fused[:], MULT)

@@ -24,31 +24,35 @@ def tile_centergeoattention_kernel(tc, base, h, w_gate, b_gate, w_fuse, b_fuse, 
         tc.psum_pool(name="psum", bufs=1) as psum,
     ):
         offsets = held.tile([P, N // 16], U16, name="offsets")
-        gate_bias = [held.tile([P, 1], F32, name=f"gate_bias{cb}") for cb in range(CB)]
-        fuse_bias = [held.tile([P, 1], F32, name=f"fuse_bias{cb}") for cb in range(CB)]
-        h_bf = [held.tile([P, N], BF16, name=f"h_bf{kb}") for kb in range(CB)]
+        gate_bias = held.tile([P, CB], F32, name="gate_bias")
+        fuse_bias = held.tile([P, CB], F32, name="fuse_bias")
+        h_half = [held.tile([P, 2, N], BF16, name=f"h_half{i}") for i in range(2)]
         gate_w = [held.tile([P, CB, P], BF16, name=f"gate_w{cb}") for cb in range(CB)]
         fuse_w = [held.tile([P, CB, P], BF16, name=f"fuse_w{cb}") for cb in range(CB)]
         window = [held.tile([P, S], F32, name=f"window{cb}") for cb in range(CB)]
 
-        def load_bias(queue, tile, bias, cb):
-            queue.dma_start(tile[:], bias[cb * P : (cb + 1) * P, :])
+        def load_bias(queue, tile, bias):
+            with nc.allow_non_contiguous_dma(reason="a bias column, one element to a partition"):
+                queue.dma_start(tile[:], bias.rearrange("(cb p) o -> p (cb o)", p=P))
+
+        def h_block(kb):
+            return h_half[kb // 2][:, kb % 2, :]
+
+        def load_h(queue, i):
+            queue.dma_start(h_half[i][:], h[2 * i * P : 2 * (i + 1) * P, :].rearrange("(j p) n -> p j n", p=P))
 
         def load_weight(queue, tile, weight, cb):
             queue.dma_start(tile[:], weight[:, cb * P : (cb + 1) * P].rearrange("(kb p) m -> p kb m", p=P))
 
+        load_h(nc.sync, 0)
         load_weight(nc.scalar, gate_w[0], w_gate, 0)
-        for kb in range(CB):
-            queue = nc.sync if kb % 2 == 0 else nc.scalar
-            queue.dma_start(h_bf[kb][:], h[kb * P : (kb + 1) * P, :])
-        load_bias(nc.sync, gate_bias[0], b_gate, 0)
+        load_h(nc.sync, 1)
+        load_bias(nc.scalar, gate_bias, b_gate)
         load_weight(nc.sync, fuse_w[0], w_fuse, 0)
-        load_bias(nc.scalar, fuse_bias[0], b_fuse, 0)
+        load_bias(nc.scalar, fuse_bias, b_fuse)
         nc.sync.dma_start(offsets[:], offs)
         nc.sync.dma_start(window[0][:], base[0:P, :])
         for cb in range(1, CB):
-            load_bias(nc.sync, gate_bias[cb], b_gate, cb)
-            load_bias(nc.sync, fuse_bias[cb], b_fuse, cb)
             load_weight(nc.sync, gate_w[cb], w_gate, cb)
             load_weight(nc.sync, fuse_w[cb], w_fuse, cb)
             nc.sync.dma_start(window[cb][:], base[cb * P : (cb + 1) * P, :])
@@ -63,14 +67,17 @@ def tile_centergeoattention_kernel(tc, base, h, w_gate, b_gate, w_fuse, b_fuse, 
         nc.gpsimd.memset(scratch[:], 0.0)
         nc.scalar.activation(scratch[:], scratch[:], SILU)
 
+        half_gate_bias = held.tile([P, CB], F32, name="half_gate_bias")
+        nc.vector.tensor_scalar_mul(half_gate_bias[:], gate_bias[:], 0.5)
+
         h_f32 = []
         for cb in range(CB):
             h_f32.append(held.tile([P, N], F32, name=f"h_f32_{cb}"))
-            nc.vector.tensor_copy(h_f32[cb][:], h_bf[cb][:])
+            nc.vector.tensor_copy(h_f32[cb][:], h_block(cb))
 
         def product(acc, weight_block):
             for kb in range(CB):
-                nc.tensor.matmul(acc[:], weight_block[:, kb, :], h_bf[kb][:], start=kb == 0, stop=kb == CB - 1)
+                nc.tensor.matmul(acc[:], weight_block[:, kb, :], h_block(kb), start=kb == 0, stop=kb == CB - 1)
 
         for cb in range(CB):
             gate_ps = psum.tile([P, N], F32, name="gate_ps")
@@ -78,14 +85,12 @@ def tile_centergeoattention_kernel(tc, base, h, w_gate, b_gate, w_fuse, b_fuse, 
             fuse_ps = psum.tile([P, N], F32, name="fuse_ps")
             product(fuse_ps, fuse_w[cb])
 
-            half_gate_bias = work.tile([P, 1], F32, name="half_gate_bias")
-            nc.scalar.mul(half_gate_bias[:], gate_bias[cb][:], 0.5)
             gate_tanh = work.tile([P, N], F32, name="gate_tanh")
             half_gate = work.tile([P, N], F32, name="half_gate")
             fused = work.tile([P, N], F32, name="fused")
-            nc.scalar.activation(gate_tanh[:], gate_ps[:], TANH, bias=half_gate_bias[:], scale=0.5)
+            nc.scalar.activation(gate_tanh[:], gate_ps[:], TANH, bias=half_gate_bias[:, cb : cb + 1], scale=0.5)
             nc.scalar.activation(half_gate[:], gate_tanh[:], COPY, bias=0.25, scale=0.25)
-            nc.scalar.activation(fused[:], fuse_ps[:], SILU, bias=fuse_bias[cb][:])
+            nc.scalar.activation(fused[:], fuse_ps[:], SILU, bias=fuse_bias[:, cb : cb + 1])
 
             update = work.tile([P, N], F32, name="update")
             nc.vector.tensor_tensor(update[:], half_gate[:], fused[:], MULT)

@@ -5,7 +5,9 @@ C = 512
 S = 1024
 N = 512
 CB = C // P
-WARM_MATMULS = 5
+
+WARM_N = 256
+WARM_MATMULS = 9
 
 FLOPS = 2 * 2 * C * C * N
 
@@ -31,15 +33,15 @@ def tile_centergeoattention_kernel(tc, base, h, w_gate, b_gate, w_fuse, b_fuse, 
         fuse_w = [held.tile([P, CB, P], BF16, name=f"fuse_w{cb}") for cb in range(CB)]
         window = [held.tile([P, S], F32, name=f"window{cb}") for cb in range(CB)]
 
-        def load_bias(queue, tile, bias):
-            with nc.allow_non_contiguous_dma(reason="a bias column, one element to a partition"):
-                queue.dma_start(tile[:], bias.rearrange("(cb p) o -> p (cb o)", p=P))
-
         def h_block(kb):
             return h_half[kb // 2][:, kb % 2, :]
 
         def load_h(queue, i):
             queue.dma_start(h_half[i][:], h[2 * i * P : 2 * (i + 1) * P, :].rearrange("(j p) n -> p j n", p=P))
+
+        def load_bias(queue, tile, bias):
+            with nc.allow_non_contiguous_dma(reason="a bias column, one element to a partition"):
+                queue.dma_start(tile[:], bias.rearrange("(cb p) o -> p (cb o)", p=P))
 
         def load_weight(queue, tile, weight, cb):
             queue.dma_start(tile[:], weight[:, cb * P : (cb + 1) * P].rearrange("(kb p) m -> p kb m", p=P))
@@ -57,16 +59,16 @@ def tile_centergeoattention_kernel(tc, base, h, w_gate, b_gate, w_fuse, b_fuse, 
             load_weight(nc.sync, fuse_w[cb], w_fuse, cb)
             nc.sync.dma_start(window[cb][:], base[cb * P : (cb + 1) * P, :])
 
-        zeros = held.tile([P, N], BF16, name="zeros")
-        nc.gpsimd.memset(zeros[:], 0.0)
-        warm_ps = psum.tile([P, N], F32, name="warm_ps")
+        zeros_f32 = held.tile([P, WARM_N // 2], F32, name="zeros_f32")
+        nc.gpsimd.memset(zeros_f32[:], 0.0)
+        zeros = zeros_f32[:].bitcast(BF16)
+        warm_ps = psum.tile([P, WARM_N], F32, name="warm_ps")
         for i in range(WARM_MATMULS):
-            nc.tensor.matmul(warm_ps[:], zeros[:, 0:P], zeros[:], start=True, stop=True)
+            nc.tensor.matmul(warm_ps[:], zeros[:, 0:P], zeros, start=True, stop=True)
 
         scratch = held.tile([P, 1], F32, name="scratch")
         nc.gpsimd.memset(scratch[:], 0.0)
         nc.scalar.activation(scratch[:], scratch[:], SILU)
-
         half_gate_bias = held.tile([P, CB], F32, name="half_gate_bias")
         nc.vector.tensor_scalar_mul(half_gate_bias[:], gate_bias[:], 0.5)
 
@@ -79,6 +81,11 @@ def tile_centergeoattention_kernel(tc, base, h, w_gate, b_gate, w_fuse, b_fuse, 
             for kb in range(CB):
                 nc.tensor.matmul(acc[:], weight_block[:, kb, :], h_block(kb), start=kb == 0, stop=kb == CB - 1)
 
+        def scatter(cb, update):
+            nc.vector.tensor_tensor(window[cb][:].indirect(offsets[:]), h_f32[cb][:], update[:], ADD)
+            nc.sync.dma_start(out[cb * P : (cb + 1) * P, :], window[cb][:])
+
+        updates = []
         for cb in range(CB):
             gate_ps = psum.tile([P, N], F32, name="gate_ps")
             product(gate_ps, gate_w[cb])
@@ -94,6 +101,7 @@ def tile_centergeoattention_kernel(tc, base, h, w_gate, b_gate, w_fuse, b_fuse, 
 
             update = work.tile([P, N], F32, name="update")
             nc.vector.tensor_tensor(update[:], half_gate[:], fused[:], MULT)
-
-            nc.vector.tensor_tensor(window[cb][:].indirect(offsets[:]), h_f32[cb][:], update[:], ADD)
-            nc.sync.dma_start(out[cb * P : (cb + 1) * P, :], window[cb][:])
+            updates.append(update)
+            if cb > 0:
+                scatter(cb - 1, updates[cb - 1])
+        scatter(CB - 1, updates[CB - 1])

@@ -5,6 +5,7 @@ C = 512
 S = 1024
 N = 512
 CB = C // P
+HALF = N // 2
 
 WARM_N = 256
 WARM_MATMULS = 9
@@ -77,30 +78,43 @@ def tile_centergeoattention_kernel(tc, base, h, w_gate, b_gate, w_fuse, b_fuse, 
             h_f32.append(held.tile([P, N], F32, name=f"h_f32_{cb}"))
             nc.vector.tensor_copy(h_f32[cb][:], h_block(cb))
 
-        def product(acc, weight_block):
+        def product(acc, weight_block, first, width):
             for kb in range(CB):
-                nc.tensor.matmul(acc[:], weight_block[:, kb, :], h_block(kb), start=kb == 0, stop=kb == CB - 1)
+                nc.tensor.matmul(
+                    acc[:], weight_block[:, kb, :], h_block(kb)[:, first : first + width], start=kb == 0, stop=kb == CB - 1
+                )
 
         def scatter(cb, update):
             nc.vector.tensor_tensor(window[cb][:].indirect(offsets[:]), h_f32[cb][:], update[:], ADD)
             nc.sync.dma_start(out[cb * P : (cb + 1) * P, :], window[cb][:])
 
+        def make_half_gate(cb, half_gate):
+            gate_ps = psum.tile([P, N], F32, name="gate_ps")
+            product(gate_ps, gate_w[cb], 0, N)
+            gate_tanh = work.tile([P, N], F32, name="gate_tanh")
+            nc.scalar.activation(gate_tanh[:], gate_ps[:], TANH, bias=half_gate_bias[:, cb : cb + 1], scale=0.5)
+            if cb == 0:
+                nc.vector.tensor_scalar(half_gate[:], gate_tanh[:], 0.25, 0.25, MULT, ADD)
+            else:
+                nc.scalar.activation(half_gate[:], gate_tanh[:], COPY, bias=0.25, scale=0.25)
+
+        def make_update(cb, update, half_gate, first, width):
+            fuse_ps = psum.tile([P, width], F32, name=f"fuse_ps{first // HALF}")
+            product(fuse_ps, fuse_w[cb], first, width)
+            fused = work.tile([P, width], F32, name="fused")
+            nc.scalar.activation(fused[:], fuse_ps[:], SILU, bias=fuse_bias[:, cb : cb + 1])
+            nc.vector.tensor_tensor(update[:, first : first + width], half_gate[:, first : first + width], fused[:], MULT)
+
         updates = []
         for cb in range(CB):
-            gate_ps = psum.tile([P, N], F32, name="gate_ps")
-            product(gate_ps, gate_w[cb])
-            fuse_ps = psum.tile([P, N], F32, name="fuse_ps")
-            product(fuse_ps, fuse_w[cb])
-
-            gate_tanh = work.tile([P, N], F32, name="gate_tanh")
             half_gate = work.tile([P, N], F32, name="half_gate")
-            fused = work.tile([P, N], F32, name="fused")
-            nc.scalar.activation(gate_tanh[:], gate_ps[:], TANH, bias=half_gate_bias[:, cb : cb + 1], scale=0.5)
-            nc.scalar.activation(half_gate[:], gate_tanh[:], COPY, bias=0.25, scale=0.25)
-            nc.scalar.activation(fused[:], fuse_ps[:], SILU, bias=fuse_bias[:, cb : cb + 1])
-
             update = work.tile([P, N], F32, name="update")
-            nc.vector.tensor_tensor(update[:], half_gate[:], fused[:], MULT)
+            make_half_gate(cb, half_gate)
+            if cb == 0:
+                make_update(cb, update, half_gate, 0, HALF)
+                make_update(cb, update, half_gate, HALF, HALF)
+            else:
+                make_update(cb, update, half_gate, 0, N)
             updates.append(update)
             if cb > 0:
                 scatter(cb - 1, updates[cb - 1])

@@ -5,7 +5,7 @@ C = 512
 S = 1024
 N = 512
 CB = C // P
-HALF = N // 2
+FIRST_BLOCK_PIECES = (256, 128, 64, 64)
 
 WARM_N = 256
 WARM_MATMULS = 9
@@ -88,33 +88,40 @@ def tile_centergeoattention_kernel(tc, base, h, w_gate, b_gate, w_fuse, b_fuse, 
             nc.vector.tensor_tensor(window[cb][:].indirect(offsets[:]), h_f32[cb][:], update[:], ADD)
             nc.sync.dma_start(out[cb * P : (cb + 1) * P, :], window[cb][:])
 
-        def make_half_gate(cb, half_gate):
+        def make_half_gate(cb, half_gate, pieces):
             gate_ps = psum.tile([P, N], F32, name="gate_ps")
             product(gate_ps, gate_w[cb], 0, N)
             gate_tanh = work.tile([P, N], F32, name="gate_tanh")
-            nc.scalar.activation(gate_tanh[:], gate_ps[:], TANH, bias=half_gate_bias[:, cb : cb + 1], scale=0.5)
-            if cb == 0:
-                nc.vector.tensor_scalar(half_gate[:], gate_tanh[:], 0.25, 0.25, MULT, ADD)
-            else:
-                nc.scalar.activation(half_gate[:], gate_tanh[:], COPY, bias=0.25, scale=0.25)
+            first = 0
+            for width in pieces:
+                nodes = slice(first, first + width)
+                nc.scalar.activation(
+                    gate_tanh[:, nodes], gate_ps[:, nodes], TANH, bias=half_gate_bias[:, cb : cb + 1], scale=0.5
+                )
+                if cb == 0:
+                    nc.vector.tensor_scalar(half_gate[:, nodes], gate_tanh[:, nodes], 0.25, 0.25, MULT, ADD)
+                else:
+                    nc.scalar.activation(half_gate[:, nodes], gate_tanh[:, nodes], COPY, bias=0.25, scale=0.25)
+                first += width
 
-        def make_update(cb, update, half_gate, first, width):
-            fuse_ps = psum.tile([P, width], F32, name=f"fuse_ps{first // HALF}")
+        def make_update(cb, update, half_gate, fused, piece, first, width):
+            nodes = slice(first, first + width)
+            fuse_ps = psum.tile([P, width], F32, name=f"fuse_ps{piece}")
             product(fuse_ps, fuse_w[cb], first, width)
-            fused = work.tile([P, width], F32, name="fused")
-            nc.scalar.activation(fused[:], fuse_ps[:], SILU, bias=fuse_bias[:, cb : cb + 1])
-            nc.vector.tensor_tensor(update[:, first : first + width], half_gate[:, first : first + width], fused[:], MULT)
+            nc.scalar.activation(fused[:, nodes], fuse_ps[:], SILU, bias=fuse_bias[:, cb : cb + 1])
+            nc.vector.tensor_tensor(update[:, nodes], half_gate[:, nodes], fused[:, nodes], MULT)
 
         updates = []
         for cb in range(CB):
             half_gate = work.tile([P, N], F32, name="half_gate")
+            fused = work.tile([P, N], F32, name="fused")
             update = work.tile([P, N], F32, name="update")
-            make_half_gate(cb, half_gate)
-            if cb == 0:
-                make_update(cb, update, half_gate, 0, HALF)
-                make_update(cb, update, half_gate, HALF, HALF)
-            else:
-                make_update(cb, update, half_gate, 0, N)
+            pieces = FIRST_BLOCK_PIECES if cb == 0 else (N,)
+            make_half_gate(cb, half_gate, pieces)
+            first = 0
+            for piece, width in enumerate(pieces):
+                make_update(cb, update, half_gate, fused, piece, first, width)
+                first += width
             updates.append(update)
             if cb > 0:
                 scatter(cb - 1, updates[cb - 1])

@@ -5,7 +5,8 @@ C = 512
 S = 1024
 N = 512
 CB = C // P
-FIRST_BLOCK_PIECES = (256, 128, 64, 64)
+FIRST_GATE_PIECES = (256, 256)
+FIRST_FUSE_PIECES = (256, 128, 64, 64)
 
 WARM_N = 256
 WARM_MATMULS = 9
@@ -54,11 +55,11 @@ def tile_centergeoattention_kernel(tc, base, h, w_gate, b_gate, w_fuse, b_fuse, 
         load_weight(nc.sync, fuse_w[0], w_fuse, 0)
         load_bias(nc.scalar, fuse_bias, b_fuse)
         nc.sync.dma_start(offsets[:], offs)
-        nc.sync.dma_start(window[0][:], base[0:P, :])
         for cb in range(1, CB):
             load_weight(nc.sync, gate_w[cb], w_gate, cb)
+            nc.sync.dma_start(window[cb - 1][:], base[(cb - 1) * P : cb * P, :])
             load_weight(nc.sync, fuse_w[cb], w_fuse, cb)
-            nc.sync.dma_start(window[cb][:], base[cb * P : (cb + 1) * P, :])
+        nc.sync.dma_start(window[CB - 1][:], base[(CB - 1) * P : C, :])
 
         zeros_f32 = held.tile([P, WARM_N // 2], F32, name="zeros_f32")
         nc.gpsimd.memset(zeros_f32[:], 0.0)
@@ -85,18 +86,18 @@ def tile_centergeoattention_kernel(tc, base, h, w_gate, b_gate, w_fuse, b_fuse, 
                 )
 
         def scatter(cb, update):
-            nc.vector.tensor_tensor(window[cb][:].indirect(offsets[:]), h_f32[cb][:], update[:], ADD)
+            nc.vector.tensor_tensor(window[cb][:].indirect(offsets[:]), h_f32[cb][:], update, ADD)
             nc.sync.dma_start(out[cb * P : (cb + 1) * P, :], window[cb][:])
 
         def make_half_gate(cb, half_gate, pieces):
-            gate_ps = psum.tile([P, N], F32, name="gate_ps")
-            product(gate_ps, gate_w[cb], 0, N)
             gate_tanh = work.tile([P, N], F32, name="gate_tanh")
             first = 0
-            for width in pieces:
+            for piece, width in enumerate(pieces):
                 nodes = slice(first, first + width)
+                gate_ps = psum.tile([P, width], F32, name=f"gate_ps{piece}")
+                product(gate_ps, gate_w[cb], first, width)
                 nc.scalar.activation(
-                    gate_tanh[:, nodes], gate_ps[:, nodes], TANH, bias=half_gate_bias[:, cb : cb + 1], scale=0.5
+                    gate_tanh[:, nodes], gate_ps[:], TANH, bias=half_gate_bias[:, cb : cb + 1], scale=0.5
                 )
                 if cb == 0:
                     nc.vector.tensor_scalar(half_gate[:, nodes], gate_tanh[:, nodes], 0.25, 0.25, MULT, ADD)
@@ -104,25 +105,38 @@ def tile_centergeoattention_kernel(tc, base, h, w_gate, b_gate, w_fuse, b_fuse, 
                     nc.scalar.activation(half_gate[:, nodes], gate_tanh[:, nodes], COPY, bias=0.25, scale=0.25)
                 first += width
 
-        def make_update(cb, update, half_gate, fused, piece, first, width):
+        def make_fused(cb, fused, piece, first, width):
             nodes = slice(first, first + width)
             fuse_ps = psum.tile([P, width], F32, name=f"fuse_ps{piece}")
             product(fuse_ps, fuse_w[cb], first, width)
             nc.scalar.activation(fused[:, nodes], fuse_ps[:], SILU, bias=fuse_bias[:, cb : cb + 1])
-            nc.vector.tensor_tensor(update[:, nodes], half_gate[:, nodes], fused[:, nodes], MULT)
 
-        updates = []
-        for cb in range(CB):
-            half_gate = work.tile([P, N], F32, name="half_gate")
-            fused = work.tile([P, N], F32, name="fused")
-            update = work.tile([P, N], F32, name="update")
-            pieces = FIRST_BLOCK_PIECES if cb == 0 else (N,)
-            make_half_gate(cb, half_gate, pieces)
-            first = 0
-            for piece, width in enumerate(pieces):
-                make_update(cb, update, half_gate, fused, piece, first, width)
-                first += width
-            updates.append(update)
-            if cb > 0:
-                scatter(cb - 1, updates[cb - 1])
-        scatter(CB - 1, updates[CB - 1])
+        half_gate = work.tile([P, N], F32, name="half_gate")
+        fused = work.tile([P, N], F32, name="fused")
+        first_update = held.tile([P, N], F32, name="first_update")
+        make_half_gate(0, half_gate, FIRST_GATE_PIECES)
+        first = 0
+        for piece, width in enumerate(FIRST_FUSE_PIECES):
+            nodes = slice(first, first + width)
+            make_fused(0, fused, piece, first, width)
+            nc.vector.tensor_tensor(first_update[:, nodes], half_gate[:, nodes], fused[:, nodes], MULT)
+            first += width
+
+        half_gate = work.tile([P, N], F32, name="half_gate")
+        fused = work.tile([P, N], F32, name="fused")
+        second_update = held.tile([P, N], F32, name="second_update")
+        make_half_gate(1, half_gate, (N,))
+        make_fused(1, fused, 0, 0, N)
+        nc.vector.tensor_tensor(second_update[:], half_gate[:], fused[:], MULT)
+        scatter(0, first_update[:])
+
+        pair_half_gate = held.tile([P, 2, N], F32, name="pair_half_gate")
+        pair_fused = held.tile([P, 2, N], F32, name="pair_fused")
+        pair_update = held.tile([P, 2, N], F32, name="pair_update")
+        for i in range(2):
+            make_half_gate(2 + i, pair_half_gate[:, i, :], (N,))
+            make_fused(2 + i, pair_fused[:, i, :], 0, 0, N)
+        scatter(1, second_update[:])
+        nc.vector.tensor_tensor(pair_update[:], pair_half_gate[:], pair_fused[:], MULT)
+        for i in range(2):
+            scatter(2 + i, pair_update[:, i, :])

@@ -28,8 +28,10 @@ def tile_centergeoattention_kernel(tc, base, h, w_gate, b_gate, w_fuse, b_fuse, 
         tc.psum_pool(name="psum", bufs=1) as psum,
     ):
         offsets = held.tile([P, N // 16], U16, name="offsets")
-        gate_bias = held.tile([P, CB], F32, name="gate_bias")
-        fuse_bias = held.tile([P, CB], F32, name="fuse_bias")
+        gate_bias_first = held.tile([P, 1], F32, name="gate_bias_first")
+        fuse_bias_first = held.tile([P, 1], F32, name="fuse_bias_first")
+        gate_bias_others = held.tile([P, CB - 1], F32, name="gate_bias_others")
+        fuse_bias_others = held.tile([P, CB - 1], F32, name="fuse_bias_others")
         h_half = [held.tile([P, 2, N], BF16, name=f"h_half{i}") for i in range(2)]
         gate_w = [held.tile([P, CB, P], BF16, name=f"gate_w{cb}") for cb in range(CB)]
         fuse_w = [held.tile([P, CB, P], BF16, name=f"fuse_w{cb}") for cb in range(CB)]
@@ -51,14 +53,18 @@ def tile_centergeoattention_kernel(tc, base, h, w_gate, b_gate, w_fuse, b_fuse, 
         load_h(nc.sync, 0)
         load_weight(nc.scalar, gate_w[0], w_gate, 0)
         load_h(nc.sync, 1)
-        load_bias(nc.scalar, gate_bias, b_gate)
+        load_bias(nc.scalar, gate_bias_first, b_gate[0:P, :])
         load_weight(nc.sync, fuse_w[0], w_fuse, 0)
-        load_bias(nc.scalar, fuse_bias, b_fuse)
+        load_bias(nc.scalar, fuse_bias_first, b_fuse[0:P, :])
         nc.sync.dma_start(offsets[:], offs)
         for cb in range(1, CB):
             load_weight(nc.sync, gate_w[cb], w_gate, cb)
+            if cb == 1:
+                load_bias(nc.sync, gate_bias_others, b_gate[P:C, :])
             nc.sync.dma_start(window[cb - 1][:], base[(cb - 1) * P : cb * P, :])
             load_weight(nc.sync, fuse_w[cb], w_fuse, cb)
+            if cb == 1:
+                load_bias(nc.sync, fuse_bias_others, b_fuse[P:C, :])
         nc.sync.dma_start(window[CB - 1][:], base[(CB - 1) * P : C, :])
 
         zeros_f32 = held.tile([P, WARM_N // 2], F32, name="zeros_f32")
@@ -71,8 +77,13 @@ def tile_centergeoattention_kernel(tc, base, h, w_gate, b_gate, w_fuse, b_fuse, 
         scratch = held.tile([P, 1], F32, name="scratch")
         nc.gpsimd.memset(scratch[:], 0.0)
         nc.scalar.activation(scratch[:], scratch[:], SILU)
-        half_gate_bias = held.tile([P, CB], F32, name="half_gate_bias")
-        nc.vector.tensor_scalar_mul(half_gate_bias[:], gate_bias[:], 0.5)
+        half_bias_first = held.tile([P, 1], F32, name="half_bias_first")
+        nc.vector.tensor_scalar_mul(half_bias_first[:], gate_bias_first[:], 0.5)
+        half_bias_others = held.tile([P, CB - 1], F32, name="half_bias_others")
+        nc.gpsimd.tensor_scalar_mul(half_bias_others[:], gate_bias_others[:], 0.5)
+
+        def bias_column(first_block, other_blocks, cb):
+            return first_block[:] if cb == 0 else other_blocks[:, cb - 1 : cb]
 
         h_f32 = []
         for cb in range(CB):
@@ -96,9 +107,8 @@ def tile_centergeoattention_kernel(tc, base, h, w_gate, b_gate, w_fuse, b_fuse, 
                 nodes = slice(first, first + width)
                 gate_ps = psum.tile([P, width], F32, name=f"gate_ps{piece}")
                 product(gate_ps, gate_w[cb], first, width)
-                nc.scalar.activation(
-                    gate_tanh[:, nodes], gate_ps[:], TANH, bias=half_gate_bias[:, cb : cb + 1], scale=0.5
-                )
+                half_bias = bias_column(half_bias_first, half_bias_others, cb)
+                nc.scalar.activation(gate_tanh[:, nodes], gate_ps[:], TANH, bias=half_bias, scale=0.5)
                 if cb == 0:
                     nc.vector.tensor_scalar(half_gate[:, nodes], gate_tanh[:, nodes], 0.25, 0.25, MULT, ADD)
                 else:
@@ -109,7 +119,7 @@ def tile_centergeoattention_kernel(tc, base, h, w_gate, b_gate, w_fuse, b_fuse, 
             nodes = slice(first, first + width)
             fuse_ps = psum.tile([P, width], F32, name=f"fuse_ps{piece}")
             product(fuse_ps, fuse_w[cb], first, width)
-            nc.scalar.activation(fused[:, nodes], fuse_ps[:], SILU, bias=fuse_bias[:, cb : cb + 1])
+            nc.scalar.activation(fused[:, nodes], fuse_ps[:], SILU, bias=bias_column(fuse_bias_first, fuse_bias_others, cb))
 
         half_gate = work.tile([P, N], F32, name="half_gate")
         fused = work.tile([P, N], F32, name="fused")

@@ -140,13 +140,14 @@ def tile_centergeoattention_kernel(tc, base, h, w_gate, b_gate, w_fuse, b_fuse, 
         nc.vector.tensor_tensor(second_update[:], half_gate[:], fused[:], MULT)
         scatter(0, first_update[:])
 
-        pair_half_gate = held.tile([P, 2, N], F32, name="pair_half_gate")
-        pair_fused = held.tile([P, 2, N], F32, name="pair_fused")
-        pair_update = held.tile([P, 2, N], F32, name="pair_update")
+        pair_half_gate = held.tile([P, 2 * N], F32, name="pair_half_gate")
+        pair_fused = held.tile([P, 2 * N], F32, name="pair_fused")
+        pair_update = held.tile([P, 2 * N], F32, name="pair_update")
         for i in range(2):
-            make_half_gate(2 + i, pair_half_gate[:, i, :], (N,))
-            make_fused(2 + i, pair_fused[:, i, :], 0, 0, N)
+            make_half_gate(2 + i, pair_half_gate[:, i * N : (i + 1) * N], (N,))
+            make_fused(2 + i, pair_fused[:, i * N : (i + 1) * N], 0, 0, N)
         scatter(1, second_update[:])
-        nc.vector.tensor_tensor(pair_update[:], pair_half_gate[:], pair_fused[:], MULT)
+        for columns in (slice(0, N + N // 2), slice(N + N // 2, 2 * N)):
+            nc.vector.tensor_tensor(pair_update[:, columns], pair_half_gate[:, columns], pair_fused[:, columns], MULT)
         for i in range(2):
-            scatter(2 + i, pair_update[:, i, :])
+            scatter(2 + i, pair_update[:, i * N : (i + 1) * N])

@@ -5,7 +5,6 @@ C = 512
 S = 1024
 N = 512
 CB = C // P
-FIRST_GATE_PIECES = (256, 256)
 FIRST_FUSE_PIECES = (256, 128, 64, 64)
 
 WARM_N = 256
@@ -82,49 +81,54 @@ def tile_centergeoattention_kernel(tc, base, h, w_gate, b_gate, w_fuse, b_fuse, 
         half_bias_others = held.tile([P, CB - 1], F32, name="half_bias_others")
         nc.gpsimd.tensor_scalar_mul(half_bias_others[:], gate_bias_others[:], 0.5)
 
-        def bias_column(first_block, other_blocks, cb):
-            return first_block[:] if cb == 0 else other_blocks[:, cb - 1 : cb]
-
         h_f32 = []
         for cb in range(CB):
             h_f32.append(held.tile([P, N], F32, name=f"h_f32_{cb}"))
             nc.vector.tensor_copy(h_f32[cb][:], h_block(cb))
 
+        def product_step(acc, weight_block, kb, first, width):
+            nc.tensor.matmul(
+                acc[:], weight_block[:, kb, :], h_block(kb)[:, first : first + width], start=kb == 0, stop=kb == CB - 1
+            )
+
         def product(acc, weight_block, first, width):
             for kb in range(CB):
-                nc.tensor.matmul(
-                    acc[:], weight_block[:, kb, :], h_block(kb)[:, first : first + width], start=kb == 0, stop=kb == CB - 1
-                )
+                product_step(acc, weight_block, kb, first, width)
 
         def scatter(cb, update):
             nc.vector.tensor_tensor(window[cb][:].indirect(offsets[:]), h_f32[cb][:], update, ADD)
             nc.sync.dma_start(out[cb * P : (cb + 1) * P, :], window[cb][:])
 
-        def make_half_gate(cb, half_gate, pieces):
+        def make_first_half_gate(half_gate):
             gate_tanh = work.tile([P, N], F32, name="gate_tanh")
-            first = 0
-            for piece, width in enumerate(pieces):
-                nodes = slice(first, first + width)
-                gate_ps = psum.tile([P, width], F32, name=f"gate_ps{piece}")
-                product(gate_ps, gate_w[cb], first, width)
-                half_bias = bias_column(half_bias_first, half_bias_others, cb)
-                nc.scalar.activation(gate_tanh[:, nodes], gate_ps[:], TANH, bias=half_bias, scale=0.5)
-                if cb == 0:
-                    nc.vector.tensor_scalar(half_gate[:, nodes], gate_tanh[:, nodes], 0.25, 0.25, MULT, ADD)
-                else:
-                    nc.scalar.activation(half_gate[:, nodes], gate_tanh[:, nodes], COPY, bias=0.25, scale=0.25)
-                first += width
+            width = N // 2
+            gate_ps = [psum.tile([P, width], F32, name=f"gate_ps{piece}") for piece in range(2)]
+            for half in range(2):
+                for piece in range(2):
+                    for kb in (2 * half, 2 * half + 1):
+                        product_step(gate_ps[piece], gate_w[0], kb, piece * width, width)
+            for piece in range(2):
+                nodes = slice(piece * width, (piece + 1) * width)
+                nc.scalar.activation(gate_tanh[:, nodes], gate_ps[piece][:], TANH, bias=half_bias_first[:], scale=0.5)
+                nc.vector.tensor_scalar(half_gate[:, nodes], gate_tanh[:, nodes], 0.25, 0.25, MULT, ADD)
+
+        def make_half_gate(cb, half_gate):
+            gate_tanh = work.tile([P, N], F32, name="gate_tanh")
+            gate_ps = psum.tile([P, N], F32, name="gate_ps0")
+            product(gate_ps, gate_w[cb], 0, N)
+            nc.scalar.activation(gate_tanh[:], gate_ps[:], TANH, bias=half_bias_others[:, cb - 1 : cb], scale=0.5)
+            nc.scalar.activation(half_gate, gate_tanh[:], COPY, bias=0.25, scale=0.25)
 
         def make_fused(cb, fused, piece, first, width):
             nodes = slice(first, first + width)
             fuse_ps = psum.tile([P, width], F32, name=f"fuse_ps{piece}")
             product(fuse_ps, fuse_w[cb], first, width)
-            nc.scalar.activation(fused[:, nodes], fuse_ps[:], SILU, bias=bias_column(fuse_bias_first, fuse_bias_others, cb))
+            nc.scalar.activation(fused[:, nodes], fuse_ps[:], SILU, bias=fuse_bias_first[:] if cb == 0 else fuse_bias_others[:, cb - 1 : cb])
 
         half_gate = work.tile([P, N], F32, name="half_gate")
         fused = work.tile([P, N], F32, name="fused")
         first_update = held.tile([P, N], F32, name="first_update")
-        make_half_gate(0, half_gate, FIRST_GATE_PIECES)
+        make_first_half_gate(half_gate)
         first = 0
         for piece, width in enumerate(FIRST_FUSE_PIECES):
             nodes = slice(first, first + width)
@@ -135,7 +139,7 @@ def tile_centergeoattention_kernel(tc, base, h, w_gate, b_gate, w_fuse, b_fuse, 
         half_gate = work.tile([P, N], F32, name="half_gate")
         fused = work.tile([P, N], F32, name="fused")
         second_update = held.tile([P, N], F32, name="second_update")
-        make_half_gate(1, half_gate, (N,))
+        make_half_gate(1, half_gate[:])
         make_fused(1, fused, 0, 0, N)
         nc.vector.tensor_tensor(second_update[:], half_gate[:], fused[:], MULT)
         scatter(0, first_update[:])
@@ -144,7 +148,7 @@ def tile_centergeoattention_kernel(tc, base, h, w_gate, b_gate, w_fuse, b_fuse, 
         pair_fused = held.tile([P, 2 * N], F32, name="pair_fused")
         pair_update = held.tile([P, 2 * N], F32, name="pair_update")
         for i in range(2):
-            make_half_gate(2 + i, pair_half_gate[:, i * N : (i + 1) * N], (N,))
+            make_half_gate(2 + i, pair_half_gate[:, i * N : (i + 1) * N])
             make_fused(2 + i, pair_fused[:, i * N : (i + 1) * N], 0, 0, N)
         scatter(1, second_update[:])
         for columns in (slice(0, N + N // 2), slice(N + N // 2, 2 * N)):

import concourse.mybir as mybir

P = 128
C = 512
S = 1024
N = 512
CB = C // P
FIRST_FUSE_PIECES = (256, 128, 64, 64)

WARM_N = 256
WARM_MATMULS = 9

FLOPS = 2 * 2 * C * C * N

BF16, F32, U16 = mybir.dt.bfloat16, mybir.dt.float32, mybir.dt.uint16
MULT, ADD = mybir.AluOpType.mult, mybir.AluOpType.add
TANH = mybir.ActivationFunctionType.Tanh
SILU = mybir.ActivationFunctionType.Silu
COPY = mybir.ActivationFunctionType.Copy


def tile_centergeoattention_kernel(tc, base, h, w_gate, b_gate, w_fuse, b_fuse, offs, out):
    nc = tc.nc
    with (
        tc.tile_pool(name="held", bufs=1) as held,
        tc.tile_pool(name="work", bufs=2) as work,
        tc.psum_pool(name="psum", bufs=1) as psum,
    ):
        offsets = held.tile([P, N // 16], U16, name="offsets")
        gate_bias_first = held.tile([P, 1], F32, name="gate_bias_first")
        fuse_bias_first = held.tile([P, 1], F32, name="fuse_bias_first")
        gate_bias_others = held.tile([P, CB - 1], F32, name="gate_bias_others")
        fuse_bias_others = held.tile([P, CB - 1], F32, name="fuse_bias_others")
        h_half = [held.tile([P, 2, N], BF16, name=f"h_half{i}") for i in range(2)]
        gate_w = [held.tile([P, CB, P], BF16, name=f"gate_w{cb}") for cb in range(CB)]
        fuse_w = [held.tile([P, CB, P], BF16, name=f"fuse_w{cb}") for cb in range(CB)]
        window = [held.tile([P, S], F32, name=f"window{cb}") for cb in range(CB)]

        def h_block(kb):
            return h_half[kb // 2][:, kb % 2, :]

        def load_h(queue, i):
            queue.dma_start(h_half[i][:], h[2 * i * P : 2 * (i + 1) * P, :].rearrange("(j p) n -> p j n", p=P))

        def load_bias(queue, tile, bias):
            with nc.allow_non_contiguous_dma(reason="a bias column, one element to a partition"):
                queue.dma_start(tile[:], bias.rearrange("(cb p) o -> p (cb o)", p=P))

        def load_weight(queue, tile, weight, cb):
            queue.dma_start(tile[:], weight[:, cb * P : (cb + 1) * P].rearrange("(kb p) m -> p kb m", p=P))

        load_h(nc.sync, 0)
        load_weight(nc.scalar, gate_w[0], w_gate, 0)
        load_h(nc.sync, 1)
        load_bias(nc.scalar, gate_bias_first, b_gate[0:P, :])
        load_weight(nc.sync, fuse_w[0], w_fuse, 0)
        load_bias(nc.scalar, fuse_bias_first, b_fuse[0:P, :])
        nc.sync.dma_start(offsets[:], offs)
        for cb in range(1, CB):
            load_weight(nc.sync, gate_w[cb], w_gate, cb)
            if cb == 1:
                load_bias(nc.sync, gate_bias_others, b_gate[P:C, :])
            nc.sync.dma_start(window[cb - 1][:], base[(cb - 1) * P : cb * P, :])
            load_weight(nc.sync, fuse_w[cb], w_fuse, cb)
            if cb == 1:
                load_bias(nc.sync, fuse_bias_others, b_fuse[P:C, :])
        nc.sync.dma_start(window[CB - 1][:], base[(CB - 1) * P : C, :])

        zeros_f32 = held.tile([P, WARM_N // 2], F32, name="zeros_f32")
        nc.gpsimd.memset(zeros_f32[:], 0.0)
        zeros = zeros_f32[:].bitcast(BF16)
        warm_ps = psum.tile([P, WARM_N], F32, name="warm_ps")
        for i in range(WARM_MATMULS):
            nc.tensor.matmul(warm_ps[:], zeros[:, 0:P], zeros, start=True, stop=True)

        scratch = held.tile([P, 1], F32, name="scratch")
        nc.gpsimd.memset(scratch[:], 0.0)
        nc.scalar.activation(scratch[:], scratch[:], SILU)
        half_bias_first = held.tile([P, 1], F32, name="half_bias_first")
        nc.vector.tensor_scalar_mul(half_bias_first[:], gate_bias_first[:], 0.5)
        half_bias_others = held.tile([P, CB - 1], F32, name="half_bias_others")
        nc.gpsimd.tensor_scalar_mul(half_bias_others[:], gate_bias_others[:], 0.5)

        h_f32 = []
        for cb in range(CB):
            h_f32.append(held.tile([P, N], F32, name=f"h_f32_{cb}"))
            nc.vector.tensor_copy(h_f32[cb][:], h_block(cb))

        def product_step(acc, weight_block, kb, first, width):
            nc.tensor.matmul(
                acc[:], weight_block[:, kb, :], h_block(kb)[:, first : first + width], start=kb == 0, stop=kb == CB - 1
            )

        def product(acc, weight_block, first, width):
            for kb in range(CB):
                product_step(acc, weight_block, kb, first, width)

        def scatter(cb, update):
            nc.vector.tensor_tensor(window[cb][:].indirect(offsets[:]), h_f32[cb][:], update, ADD)
            nc.sync.dma_start(out[cb * P : (cb + 1) * P, :], window[cb][:])

        def make_first_half_gate(half_gate):
            gate_tanh = work.tile([P, N], F32, name="gate_tanh")
            width = N // 2
            gate_ps = [psum.tile([P, width], F32, name=f"gate_ps{piece}") for piece in range(2)]
            for half in range(2):
                for piece in range(2):
                    for kb in (2 * half, 2 * half + 1):
                        product_step(gate_ps[piece], gate_w[0], kb, piece * width, width)
            for piece in range(2):
                nodes = slice(piece * width, (piece + 1) * width)
                nc.scalar.activation(gate_tanh[:, nodes], gate_ps[piece][:], TANH, bias=half_bias_first[:], scale=0.5)
                nc.vector.tensor_scalar(half_gate[:, nodes], gate_tanh[:, nodes], 0.25, 0.25, MULT, ADD)

        def make_half_gate(cb, half_gate):
            gate_tanh = work.tile([P, N], F32, name="gate_tanh")
            gate_ps = psum.tile([P, N], F32, name="gate_ps0")
            product(gate_ps, gate_w[cb], 0, N)
            nc.scalar.activation(gate_tanh[:], gate_ps[:], TANH, bias=half_bias_others[:, cb - 1 : cb], scale=0.5)
            nc.scalar.activation(half_gate, gate_tanh[:], COPY, bias=0.25, scale=0.25)

        def make_fused(cb, fused, piece, first, width):
            nodes = slice(first, first + width)
            fuse_ps = psum.tile([P, width], F32, name=f"fuse_ps{piece}")
            product(fuse_ps, fuse_w[cb], first, width)
            nc.scalar.activation(fused[:, nodes], fuse_ps[:], SILU, bias=fuse_bias_first[:] if cb == 0 else fuse_bias_others[:, cb - 1 : cb])

        half_gate = work.tile([P, N], F32, name="half_gate")
        fused = work.tile([P, N], F32, name="fused")
        first_update = held.tile([P, N], F32, name="first_update")
        make_first_half_gate(half_gate)
        first = 0
        for piece, width in enumerate(FIRST_FUSE_PIECES):
            nodes = slice(first, first + width)
            make_fused(0, fused, piece, first, width)
            nc.vector.tensor_tensor(first_update[:, nodes], half_gate[:, nodes], fused[:, nodes], MULT)
            first += width

        half_gate = work.tile([P, N], F32, name="half_gate")
        fused = work.tile([P, N], F32, name="fused")
        second_update = held.tile([P, N], F32, name="second_update")
        make_half_gate(1, half_gate[:])
        make_fused(1, fused, 0, 0, N)
        nc.vector.tensor_tensor(second_update[:], half_gate[:], fused[:], MULT)
        scatter(0, first_update[:])

        pair_half_gate = held.tile([P, 2 * N], F32, name="pair_half_gate")
        pair_fused = held.tile([P, 2 * N], F32, name="pair_fused")
        pair_update = held.tile([P, 2 * N], F32, name="pair_update")
        for i in range(2):
            make_half_gate(2 + i, pair_half_gate[:, i * N : (i + 1) * N])
            make_fused(2 + i, pair_fused[:, i * N : (i + 1) * N], 0, 0, N)
        scatter(1, second_update[:])
        for columns in (slice(0, N + N // 2), slice(N + N // 2, 2 * N)):
            nc.vector.tensor_tensor(pair_update[:, columns], pair_half_gate[:, columns], pair_fused[:, columns], MULT)
        for i in range(2):
            scatter(2 + i, pair_update[:, i * N : (i + 1) * N])
